import numpy as np
import ml_dtypes


def mxq(x, axis, fmt="e4m3"):
    dtype, down = {"e4m3": (ml_dtypes.float8_e4m3fn, 7), "e5m2": (ml_dtypes.float8_e5m2, 14)}[fmt]
    v = np.moveaxis(np.asarray(x, np.float32).astype(ml_dtypes.bfloat16).astype(np.float64), axis, -1)
    blocks = v.reshape(v.shape[:-1] + (-1, 32))
    amax = np.abs(blocks).max(-1, keepdims=True)
    byte = np.maximum(np.where(amax > 0, np.frexp(amax)[1] - 1 + 127, 0) - down, 1)
    scale = np.exp2(byte - 127.0)
    codes = (blocks / scale).astype(np.float32).astype(dtype).astype(np.float64)
    return np.moveaxis((codes * scale).reshape(v.shape), -1, axis)


WIDE = False


def mx_kscale(k):
    if not WIDE:
        return np.ones(k)
    levels = np.array([10, -10, 5, -5, 0])
    if k % 512:
        return np.exp2(np.random.permutation(np.resize(levels, k // 32))).repeat(32)
    a = np.empty((k // 512, 16))
    for p in range(k // 512):
        a[p, :8] = np.random.permutation(np.resize(levels, 8))
        for g in range(8):
            far = levels[np.abs(levels - a[p, g]) >= 10]
            a[p, g + 8] = far[np.random.randint(len(far))]
    return np.exp2(a.ravel()).repeat(32)


BF16 = ml_dtypes.bfloat16


def bf(x):
    return np.asarray(x, np.float32).astype(BF16)


def f64(x):
    return np.asarray(x).astype(np.float64)


B, D, H = 1024, 1024, 1024


def setup_inputs():
    s = mx_kscale(D)
    return {"h_c1": bf(np.random.standard_normal((B, H))),
            "h_c2": bf(np.random.standard_normal((B, H))),
            "x_t": bf(np.random.standard_normal((B, D)) * s),
            "r_param": bf(np.random.uniform(0.1, 1.05, (1, H))),
            "theta_param": bf(np.random.uniform(0.0, 2.0 * np.pi, (1, H))),
            "w1": bf(np.random.standard_normal((D, H)) / np.sqrt(D) / s[:, None]),
            "w2": bf(np.random.standard_normal((D, H)) / np.sqrt(D) / s[:, None])}


def reference(h_c1, h_c2, x_t, r_param, theta_param, w1, w2):
    h_c1, h_c2 = f64(h_c1), f64(h_c2)
    r, theta = f64(r_param), f64(theta_param)
    g = r * np.cos(theta)
    phi = r * np.sin(theta)
    norm = np.sqrt(np.maximum(1.0 - r * r, 0.0))
    xq = mxq(f64(x_t), 1, "e4m3")
    w_c1_x = xq @ mxq(f64(w1), 0, "e4m3")
    w_c2_x = xq @ mxq(f64(w2), 0, "e4m3")
    h_t_c1 = g * h_c1 - phi * h_c2 + norm * w_c1_x
    h_t_c2 = g * h_c2 + phi * h_c1 + norm * w_c2_x
    h_t = np.maximum(np.concatenate((h_t_c1, h_t_c2), axis=-1), 0.0)
    return (h_t_c1, h_t_c2, h_t)

@@ -1,0 +1,463 @@
+import math
+from contextlib import ExitStack
+
+import concourse.mybir as mybir
+from concourse.masks import make_identity
+
+BF16 = mybir.dt.bfloat16
+F32 = mybir.dt.float32
+U32 = mybir.dt.uint32
+U8 = mybir.dt.uint8
+FP8X4 = mybir.dt.float8_e4m3fn_x4
+ACT = mybir.ActivationFunctionType
+ALU = mybir.AluOpType
+
+FLOPS = 2 * 1024 * 1024 * 2048
+P = 128
+PI_SAFE = 3.1415925
+CHUNKS = ((0, 0), (1, 0), (0, 1), (1, 1))
+W_LATE_ENGINE = "g"
+STORE_GROUPS = ((0, 2), (2, 2), (4, 2), (6, 2), (8, 2), (10, 2), (12, 2), (14, 2))
+GROUP_RELU = "VSVSVSVS"
+STAGE_BUFS = 4
+CT_BUFS = 3
+
+
+def tile_linearrtus_kernel(
+    tc, h_c1, h_c2, x_t, r_param, theta_param, w1, w2, out_0, out_1, out_2
+):
+    nc = tc.nc
+    with ExitStack() as ctx:
+        const = ctx.enter_context(tc.tile_pool(name="const", bufs=1))
+        grp_x = ctx.enter_context(tc.tile_pool(name="grp_x", bufs=2))
+        grp_w = ctx.enter_context(tc.tile_pool(name="grp_w", bufs=4))
+        work = ctx.enter_context(tc.tile_pool(name="work", bufs=CT_BUFS))
+        stage = ctx.enter_context(tc.tile_pool(name="stage", bufs=STAGE_BUFS))
+        psum = ctx.enter_context(tc.psum_pool(name="psum", bufs=1))
+        ctx.enter_context(tc.manual_schedule())
+
+        x_sb = [const.tile([P, 2048], BF16, name="x_sb%d" % ip) for ip in range(4)]
+        h_first = [
+            [const.tile([P, 4, 512], BF16, name="h%d_first%d" % (s, jc)) for jc in range(2)]
+            for s in range(2)
+        ]
+        h_second = [const.tile([P, 4, 1024], BF16, name="h%d_second" % s) for s in range(2)]
+        w_sb = [
+            [const.tile([P, 8, 512], BF16, name="w%d_sb%d" % (m, jc)) for jc in range(2)]
+            for m in range(2)
+        ]
+        x_codes = const.tile([P, 2, 1024], U32, name="x_codes", align_bytes=64)
+        x_scales = const.tile([P, 2, 1024], U8, name="x_scales", align_bytes=64)
+        w_codes = [
+            const.tile([P, 2, 1024], U32, name="w1_codes", align_bytes=64),
+            const.tile([P, 2, 1024], U32, name="w2_codes", align_bytes=64),
+        ]
+        w_scales = [
+            const.tile([P, 2, 1024], U8, name="w1_scales", align_bytes=64),
+            const.tile([P, 2, 1024], U8, name="w2_scales", align_bytes=64),
+        ]
+        ident_bf = const.tile([P, P], BF16, name="ident_bf")
+        ident_f32 = const.tile([P, P], F32, name="ident_f32")
+        par_rows = const.tile([P, P], BF16, name="par_rows")
+        warm = const.tile([P, 8], F32, name="warm")
+        r_col = const.tile([P, 8], F32, name="r_col")
+        th_col = const.tile([P, 8], F32, name="th_col")
+        d_col = const.tile([P, 8], F32, name="d_col")
+        nd_col = const.tile([P, 8], F32, name="nd_col")
+        e_col = const.tile([P, 8], F32, name="e_col")
+        s1_col = const.tile([P, 8], F32, name="s1_col")
+        s2_col = const.tile([P, 8], F32, name="s2_col")
+        g_col = const.tile([P, 8], F32, name="g_col")
+        phi_col = const.tile([P, 8], F32, name="phi_col")
+        nphi_col = const.tile([P, 8], F32, name="nphi_col")
+        v_col = const.tile([P, 8], F32, name="v_col")
+        mask_col = const.tile([P, 8], F32, name="mask_col")
+        sq_col = const.tile([P, 8], F32, name="sq_col")
+        norm_col = const.tile([P, 8], F32, name="norm_col")
+
+        nc.vector.memset(par_rows[:], 0.0)
+        nc.vector.memset(warm[:], 0.0)
+        nc.scalar.dma_start(
+            out=par_rows[0:8, :], in_=r_param.rearrange("o (j p) -> (o j) p", p=P)
+        )
+        nc.scalar.dma_start(
+            out=par_rows[8:16, :], in_=theta_param.rearrange("o (j p) -> (o j) p", p=P)
+        )
+        nc.scalar.activation(out=warm[:], in_=warm[:], func=ACT.Sin)
+        x_rows = x_t.rearrange("(p i) k -> p (i k)", i=8)
+        h_rows = [
+            h_c1.rearrange("(p i) c -> p i c", i=8),
+            h_c2.rearrange("(p i) c -> p i c", i=8),
+        ]
+        w_in = [w1, w2]
+
+        def load_x(ip):
+            nc.sync.dma_start(out=x_sb[ip][:], in_=x_rows[:, 2048 * ip : 2048 * ip + 2048])
+
+        def load_w(jc):
+            cols = slice(512 * jc, 512 * jc + 512)
+            for m in range(2):
+                for g in range(2):
+                    nc.sync.dma_start(
+                        out=w_sb[m][jc][:, 4 * g : 4 * g + 4, :],
+                        in_=w_in[m][512 * g : 512 * g + 512, cols].rearrange(
+                            "(q e) c -> q e c", e=4
+                        ),
+                    )
+
+        def load_h_first(jc):
+            for s in range(2):
+                nc.sync.dma_start(
+                    out=h_first[s][jc][:], in_=h_rows[s][:, 0:4, 512 * jc : 512 * jc + 512]
+                )
+
+        def load_h_second():
+            for s in range(2):
+                nc.sync.dma_start(out=h_second[s][:], in_=h_rows[s][:, 4:8, :])
+
+        load_x(0)
+        load_x(1)
+        load_w(0)
+        load_x(2)
+        load_x(3)
+        load_h_first(0)
+        load_w(1)
+        load_h_second()
+        load_h_first(1)
+
+        make_identity(nc, ident_f32[:])
+        make_identity(nc, ident_bf[:])
+
+        def params_transpose():
+            par_ps = psum.tile([P, P], BF16, name="par_ps", tag="o0")
+            nc.tensor.transpose(par_ps[:], par_rows[:], ident_bf[:])
+            return par_ps
+
+        def params_angles(par_ps):
+            nc.vector.tensor_copy(out=r_col[:], in_=par_ps[:, 0:8])
+            nc.vector.tensor_copy(out=th_col[:], in_=par_ps[:, 8:16])
+            nc.vector.tensor_scalar(
+                out=d_col[:], in0=th_col[:], scalar1=-math.pi, scalar2=-PI_SAFE,
+                op0=ALU.add, op1=ALU.max,
+            )
+            nc.vector.tensor_scalar(
+                out=d_col[:], in0=d_col[:], scalar1=PI_SAFE, scalar2=None, op0=ALU.min
+            )
+            nc.vector.tensor_scalar(
+                out=nd_col[:], in0=d_col[:], scalar1=-1.0, scalar2=None, op0=ALU.mult
+            )
+            nc.vector.tensor_tensor(out=e_col[:], in0=d_col[:], in1=nd_col[:], op=ALU.max)
+            nc.vector.tensor_scalar(
+                out=e_col[:], in0=e_col[:], scalar1=-0.5 * math.pi, scalar2=None, op0=ALU.add
+            )
+            nc.vector.tensor_tensor(out=v_col[:], in0=r_col[:], in1=r_col[:], op=ALU.mult)
+            nc.vector.tensor_scalar(
+                out=v_col[:], in0=v_col[:], scalar1=-1.0, scalar2=1.0,
+                op0=ALU.mult, op1=ALU.add,
+            )
+            nc.vector.tensor_scalar(
+                out=mask_col[:], in0=v_col[:], scalar1=0.0, scalar2=None, op0=ALU.is_gt
+            )
+            nc.vector.tensor_scalar(
+                out=v_col[:], in0=v_col[:], scalar1=1e-30, scalar2=None, op0=ALU.max
+            )
+
+        def params_tables():
+            nc.scalar.activation(out=s1_col[:], in_=d_col[:], func=ACT.Sin)
+            nc.scalar.activation(out=s2_col[:], in_=e_col[:], func=ACT.Sin)
+            nc.scalar.activation(out=sq_col[:], in_=v_col[:], func=ACT.Sqrt)
+
+        def params_finish():
+            nc.vector.tensor_tensor(
+                out=nphi_col[:], in0=r_col[:], in1=s1_col[:], op=ALU.mult
+            )
+            nc.vector.tensor_scalar(
+                out=phi_col[:], in0=nphi_col[:], scalar1=-1.0, scalar2=None, op0=ALU.mult
+            )
+            nc.vector.tensor_tensor(out=g_col[:], in0=r_col[:], in1=s2_col[:], op=ALU.mult)
+            nc.vector.tensor_tensor(
+                out=norm_col[:], in0=sq_col[:], in1=mask_col[:], op=ALU.mult
+            )
+
+        x_words = [x_sb[ip][:].bitcast(F32) for ip in range(4)]
+
+        def x_transposes(bh, g, half, bank):
+            xt = psum.tile([P, 512], F32, name="xt", tag=bank)
+            for i2 in range(2):
+                for u in range(2):
+                    c0 = 512 * i2 + 256 * g + u
+                    nc.tensor.transpose(
+                        xt[:, 128 * (2 * i2 + u) : 128 * (2 * i2 + u) + 128],
+                        x_words[2 * bh + half][:, c0 : c0 + 255 : 2],
+                        ident_f32[:],
+                    )
+            return xt
+
+        def x_group_tile():
+            xg = grp_x.tile([P, 2048], BF16, name="xg", tag="xg", align_bytes=64)
+            return xg
+
+        def x_copy(xg, half, xt):
+            nc.scalar.copy(
+                out=xg[:].bitcast(F32)[:, 512 * half : 512 * half + 512].rearrange(
+                    "q (i p u) -> q i p u", i=2, p=P, u=2
+                ),
+                in_=xt[:].rearrange("q (i u p) -> q i p u", i=2, u=2, p=P),
+            )
+
+        def x_quant(bh, g, xg):
+            cols = slice(512 * bh, 512 * bh + 512)
+            nc.vector.quantize_mx(
+                out=x_codes[:, g, cols].bitcast(FP8X4),
+                scales=x_scales[:, g, cols],
+                in_=xg[:],
+            )
+
+        def w_copy(m, g, jc, engine):
+            wg = grp_w.tile([P, 512, 4], BF16, name="wg", tag="wg", align_bytes=64)
+            dst = wg[:].rearrange("p (c i) t -> p c t i", i=4)
+            src = w_sb[m][jc][:, 4 * g : 4 * g + 4, :].rearrange("p t (c i) -> p c t i", i=4)
+            if engine == "v":
+                nc.vector.tensor_copy(out=dst, in_=src)
+            elif engine == "s":
+                nc.scalar.copy(out=dst, in_=src)
+            else:
+                nc.gpsimd.tensor_scalar(
+                    out=dst, in0=src, scalar1=1.0, scalar2=0.0, op0=ALU.mult, op1=ALU.add
+                )
+            return wg
+
+        def w_quant(m, g, jc, wg):
+            cols = slice(512 * jc, 512 * jc + 512)
+            nc.vector.quantize_mx(
+                out=w_codes[m][:, g, cols].bitcast(FP8X4),
+                scales=w_scales[m][:, g, cols],
+                in_=wg[:].rearrange("p c t -> p (c t)"),
+            )
+
+        units = [(c, m, jp) for c in range(4) for m in range(2) for jp in range(2)]
+        n_units = len(units)
+        ht_of = {}
+        mm_of = {}
+        ct_of = {}
+        ot_of = {}
+        st_of = {}
+
+        def lane_block(k, a):
+            c, m, jp = units[k]
+            return 4 * CHUNKS[c][1] + 2 * jp + a
+
+        def h_block(s, bh, il, j):
+            if bh == 0:
+                return h_first[s][j // 4][:, il, 128 * (j % 4) : 128 * (j % 4) + 128]
+            return h_second[s][:, il, 128 * j : 128 * j + 128]
+
+        def h_transposes(c, jl):
+            bh, jc = CHUNKS[c]
+            ht = psum.tile([P, 2, 512], BF16, name="ht", tag="h%d" % jl)
+            for s in range(2):
+                for il in range(4):
+                    nc.tensor.transpose(
+                        ht[:, s, 128 * il : 128 * il + 128],
+                        h_block(s, bh, il, 4 * jc + jl),
+                        ident_bf[:],
+                    )
+            ht_of[(c, jl)] = ht
+
+        def mx_passes(k, a):
+            c, m, jp = units[k]
+            bh = CHUNKS[c][0]
+            j = lane_block(k, a)
+            h_cols = slice(128 * j, 128 * j + 128)
+            b_cols = slice(512 * bh, 512 * bh + 512)
+            mm = psum.tile([P, 512], F32, name="mm", tag="m%d" % a)
+            for g in range(2):
+                nc.tensor.matmul_mx(
+                    out=mm[:],
+                    lhsT=w_codes[m][:, g, h_cols].bitcast(FP8X4),
+                    lhsT_scale=w_scales[m][:, g, h_cols],
+                    rhs=x_codes[:, g, b_cols].bitcast(FP8X4),
+                    rhs_scale=x_scales[:, g, b_cols],
+                    start=(g == 0),
+                    stop=(g == 1),
+                )
+            mm_of[(k, a)] = mm
+
+        def scale_out(k, a):
+            j = lane_block(k, a)
+            ct = work.tile([P, 512], F32, name="ct%d" % a, tag="ct%d" % a)
+            nc.scalar.activation(
+                out=ct[:], in_=mm_of[(k, a)][:], func=ACT.Copy, scale=norm_col[:, j : j + 1]
+            )
+            ct_of[(k, a)] = ct
+
+        plan = (((0, g_col), (1, nphi_col)), ((1, g_col), (0, phi_col)))
+
+        def rotate_add(k):
+            c, m, jp = units[k]
+            for s, coef in plan[m]:
+                for a in range(2):
+                    j = lane_block(k, a)
+                    ct = ct_of[(k, a)]
+                    nc.vector.scalar_tensor_tensor(
+                        out=ct[:], in0=ht_of[(c, 2 * jp + a)][:, s, :],
+                        scalar=coef[:, j : j + 1], in1=ct[:], op0=ALU.mult, op1=ALU.add,
+                    )
+
+        def back_transposes(k, a):
+            ot = psum.tile([P, 4, P], F32, name="ot", tag="o%d" % a)
+            for il in range(4):
+                nc.tensor.transpose(
+                    ot[:, il, :], ct_of[(k, a)][:, 128 * il : 128 * il + 128], ident_f32[:]
+                )
+            ot_of[(k, a)] = ot
+
+        group_of = {}
+        for index, (first, count) in enumerate(STORE_GROUPS):
+            for k in range(first, first + count):
+                group_of[k] = (first, count, GROUP_RELU[index])
+
+        def stage_tiles(k):
+            first, count, who = group_of[k]
+            if first not in st_of:
+                st_of[first] = [
+                    stage.tile([P, 4, 256 * count], F32, name="st_c", tag="c"),
+                    stage.tile([P, 4, 256 * count], F32, name="st_r", tag="r"),
+                ]
+            return st_of[first]
+
+        def stage_cols(k, a):
+            lo = 128 * (2 * (k - group_of[k][0]) + a)
+            return slice(lo, lo + 128)
+
+        def scalar_out(k):
+            st_c, st_r = stage_tiles(k)
+            if k == n_units - 1:
+                cols = stage_cols(k, 0)
+                nc.scalar.copy(out=st_c[:, :, cols], in_=ot_of[(k, 0)][:])
+                nc.scalar.activation(out=st_r[:, :, cols], in_=ot_of[(k, 0)][:], func=ACT.Relu)
+                return
+            for a in range(2):
+                cols = stage_cols(k, a)
+                nc.scalar.copy(out=st_c[:, :, cols], in_=ot_of[(k, a)][:])
+                if group_of[k][2] == "S":
+                    nc.scalar.activation(
+                        out=st_r[:, :, cols], in_=ot_of[(k, a)][:], func=ACT.Relu
+                    )
+
+        def vector_out(k):
+            first, count, who = group_of[k]
+            st_c, st_r = stage_tiles(k)
+            if k == n_units - 1:
+                cols = stage_cols(k, 1)
+                nc.vector.tensor_copy(out=st_c[:, :, cols], in_=ot_of[(k, 1)][:])
+                nc.vector.tensor_scalar(
+                    out=st_r[:, :, cols], in0=ot_of[(k, 1)][:],
+                    scalar1=0.0, scalar2=None, op0=ALU.max,
+                )
+            elif who == "V" and k == first + count - 1:
+                nc.vector.tensor_scalar(
+                    out=st_r[:], in0=st_c[:], scalar1=0.0, scalar2=None, op0=ALU.max
+                )
+
+        c_rows = [
+            out_0.rearrange("(p i) c -> p i c", i=8),
+            out_1.rearrange("(p i) c -> p i c", i=8),
+        ]
+        r_rows = out_2.rearrange("(p i) c -> p i c", i=8)
+
+        def stores(k):
+            first, count, who = group_of[k]
+            if k != first + count - 1:
+                return
+            c, m, jp = units[first]
+            bh = CHUNKS[c][0]
+            base = 128 * lane_block(first, 0)
+            st_c, st_r = stage_tiles(k)
+            rows = slice(4 * bh, 4 * bh + 4)
+            nc.sync.dma_start(out=c_rows[m][:, rows, base : base + 256 * count], in_=st_c[:])
+            nc.sync.dma_start(
+                out=r_rows[:, rows, 1024 * m + base : 1024 * m + base + 256 * count], in_=st_r[:]
+            )
+
+        xt_a = x_transposes(0, 0, 0, "m0")
+        xt_c = x_transposes(0, 1, 0, "h0")
+        xt_b = x_transposes(0, 0, 1, "m1")
+        xt_d = x_transposes(0, 1, 1, "h1")
+        par_ps = params_transpose()
+        xg00 = x_group_tile()
+        xg01 = x_group_tile()
+        x_copy(xg00, 0, xt_a)
+        x_copy(xg01, 0, xt_c)
+        x_copy(xg00, 1, xt_b)
+        x_copy(xg01, 1, xt_d)
+        wg_a = w_copy(0, 0, 0, "v")
+        params_angles(par_ps)
+        params_tables()
+        x_quant(0, 0, xg00)
+        w_quant(0, 0, 0, wg_a)
+        wg_b = w_copy(0, 1, 0, "s")
+        wg_c = w_copy(1, 0, 0, "v")
+        x_quant(0, 1, xg01)
+        params_finish()
+        wg_d = w_copy(1, 1, 0, "v")
+        w_quant(0, 1, 0, wg_b)
+        w_quant(1, 0, 0, wg_c)
+        w_quant(1, 1, 0, wg_d)
+
+        xt_a = x_transposes(1, 0, 0, "o0")
+        xt_b = x_transposes(1, 0, 1, "o1")
+        mx_passes(0, 0)
+        mx_passes(0, 1)
+        h_transposes(0, 0)
+        h_transposes(0, 1)
+        xg10 = x_group_tile()
+        x_copy(xg10, 0, xt_a)
+        x_copy(xg10, 1, xt_b)
+        scale_out(0, 0)
+        scale_out(0, 1)
+        mx_passes(1, 0)
+        mx_passes(1, 1)
+        h_transposes(0, 2)
+        h_transposes(0, 3)
+        xt_c = x_transposes(1, 1, 0, "o0")
+        xt_d = x_transposes(1, 1, 1, "o1")
+        scale_out(1, 0)
+        scale_out(1, 1)
+        xg11 = x_group_tile()
+        x_copy(xg11, 0, xt_c)
+        x_copy(xg11, 1, xt_d)
+        x_quant(1, 0, xg10)
+
+        late = ((0, 0), (0, 1), (1, 0), (1, 1))
+        late_wg = {}
+        for t in range(n_units + 1):
+            if t >= 1:
+                if t + 1 < n_units:
+                    mx_passes(t + 1, 0)
+                    mx_passes(t + 1, 1)
+                back_transposes(t - 1, 0)
+                back_transposes(t - 1, 1)
+                c, m, jp = units[t - 1]
+                if m == 1 and c + 1 < 4:
+                    h_transposes(c + 1, 2 * jp)
+                    h_transposes(c + 1, 2 * jp + 1)
+                if t + 1 < n_units:
+                    scale_out(t + 1, 0)
+                    scale_out(t + 1, 1)
+                scalar_out(t - 1)
+            if 2 <= t <= 5:
+                late_wg[t - 2] = w_copy(late[t - 2][0], late[t - 2][1], 1, W_LATE_ENGINE)
+            if t < n_units:
+                rotate_add(t)
+            if t == 1:
+                x_quant(1, 1, xg11)
+            if 3 <= t <= 5:
+                w_quant(late[t - 3][0], late[t - 3][1], 1, late_wg[t - 3])
+            if t == 5:
+                w_quant(late[3][0], late[3][1], 1, late_wg[3])
+            done = [t - 2] if t < n_units else [t - 2, t - 1]
+            for k in done:
+                if k >= 0:
+                    vector_out(k)
+                    stores(k)

@@ -257,11 +257,20 @@ def tile_linearrtus_kernel(
             ht = psum.tile([P, 2, 512], BF16, name="ht", tag="h%d" % jl)
             for s in range(2):
                 for il in range(4):
-                    nc.tensor.transpose(
-                        ht[:, s, 128 * il : 128 * il + 128],
-                        h_block(s, bh, il, 4 * jc + jl),
-                        ident_bf[:],
-                    )
+                    if c < 3:
+                        nc.tensor.matmul(
+                            ht[:, s, 128 * il : 128 * il + 128],
+                            lhsT=h_block(s, bh, il, 4 * jc + jl),
+                            rhs=ident_bf[:],
+                            start=True,
+                            stop=True,
+                        )
+                    else:
+                        nc.tensor.transpose(
+                            ht[:, s, 128 * il : 128 * il + 128],
+                            h_block(s, bh, il, 4 * jc + jl),
+                            ident_bf[:],
+                        )
             ht_of[(c, jl)] = ht
 
         def mx_passes(k, a):

@@ -77,12 +77,6 @@ def tile_linearrtus_kernel(
 
         nc.vector.memset(par_rows[:], 0.0)
         nc.vector.memset(warm[:], 0.0)
-        nc.scalar.dma_start(
-            out=par_rows[0:8, :], in_=r_param.rearrange("o (j p) -> (o j) p", p=P)
-        )
-        nc.scalar.dma_start(
-            out=par_rows[8:16, :], in_=theta_param.rearrange("o (j p) -> (o j) p", p=P)
-        )
         nc.scalar.activation(out=warm[:], in_=warm[:], func=ACT.Sin)
         x_rows = x_t.rearrange("(p i) k -> p (i k)", i=8)
         h_rows = [
@@ -93,6 +87,14 @@ def tile_linearrtus_kernel(
 
         def load_x(ip):
             nc.sync.dma_start(out=x_sb[ip][:], in_=x_rows[:, 2048 * ip : 2048 * ip + 2048])
+
+        def load_params():
+            nc.sync.dma_start(
+                out=par_rows[0:8, :], in_=r_param.rearrange("o (j p) -> (o j) p", p=P)
+            )
+            nc.sync.dma_start(
+                out=par_rows[8:16, :], in_=theta_param.rearrange("o (j p) -> (o j) p", p=P)
+            )
 
         def load_w(jc):
             cols = slice(512 * jc, 512 * jc + 512)
@@ -116,6 +118,7 @@ def tile_linearrtus_kernel(
                 nc.sync.dma_start(out=h_second[s][:], in_=h_rows[s][:, 4:8, :])
 
         load_x(0)
+        load_params()
         load_x(1)
         load_w(0)
         load_x(2)
@@ -391,9 +394,10 @@ def tile_linearrtus_kernel(
 
         xt_a = x_transposes(0, 0, 0, "m0")
         xt_c = x_transposes(0, 1, 0, "h0")
+        par_ps = params_transpose()
         xt_b = x_transposes(0, 0, 1, "m1")
         xt_d = x_transposes(0, 1, 1, "h1")
-        par_ps = params_transpose()
+        params_angles(par_ps)
         xg00 = x_group_tile()
         xg01 = x_group_tile()
         x_copy(xg00, 0, xt_a)
@@ -401,16 +405,15 @@ def tile_linearrtus_kernel(
         x_copy(xg00, 1, xt_b)
         x_copy(xg01, 1, xt_d)
         wg_a = w_copy(0, 0, 0, "v")
-        params_angles(par_ps)
+        wg_b = w_copy(0, 1, 0, "s")
         params_tables()
         x_quant(0, 0, xg00)
         w_quant(0, 0, 0, wg_a)
-        wg_b = w_copy(0, 1, 0, "s")
         wg_c = w_copy(1, 0, 0, "v")
         x_quant(0, 1, xg01)
+        w_quant(0, 1, 0, wg_b)
         params_finish()
         wg_d = w_copy(1, 1, 0, "v")
-        w_quant(0, 1, 0, wg_b)
         w_quant(1, 0, 0, wg_c)
         w_quant(1, 1, 0, wg_d)
 

@@ -61,9 +61,7 @@ def tile_linearrtus_kernel(
         par_rows = const.tile([P, P], BF16, name="par_rows")
         warm = const.tile([P, 8], F32, name="warm")
         r_col = const.tile([P, 8], F32, name="r_col")
-        th_col = const.tile([P, 8], F32, name="th_col")
         d_col = const.tile([P, 8], F32, name="d_col")
-        nd_col = const.tile([P, 8], F32, name="nd_col")
         e_col = const.tile([P, 8], F32, name="e_col")
         s1_col = const.tile([P, 8], F32, name="s1_col")
         s2_col = const.tile([P, 8], F32, name="s2_col")
@@ -138,31 +136,29 @@ def tile_linearrtus_kernel(
 
         def params_angles(par_ps):
             nc.vector.tensor_copy(out=r_col[:], in_=par_ps[:, 0:8])
-            nc.vector.tensor_copy(out=th_col[:], in_=par_ps[:, 8:16])
             nc.vector.tensor_scalar(
-                out=d_col[:], in0=th_col[:], scalar1=-math.pi, scalar2=-PI_SAFE,
+                out=d_col[:], in0=par_ps[:, 8:16], scalar1=-math.pi, scalar2=-PI_SAFE,
                 op0=ALU.add, op1=ALU.max,
+            )
+            nc.vector.tensor_scalar(
+                out=v_col[:], in0=r_col[:], scalar1=-1.0, scalar2=None, op0=ALU.mult
             )
             nc.vector.tensor_scalar(
                 out=d_col[:], in0=d_col[:], scalar1=PI_SAFE, scalar2=None, op0=ALU.min
             )
-            nc.vector.tensor_scalar(
-                out=nd_col[:], in0=d_col[:], scalar1=-1.0, scalar2=None, op0=ALU.mult
+            nc.vector.tensor_tensor(out=v_col[:], in0=v_col[:], in1=r_col[:], op=ALU.mult)
+            nc.vector.scalar_tensor_tensor(
+                out=e_col[:], in0=d_col[:], scalar=-1.0, in1=d_col[:], op0=ALU.mult, op1=ALU.max
             )
-            nc.vector.tensor_tensor(out=e_col[:], in0=d_col[:], in1=nd_col[:], op=ALU.max)
+            nc.vector.tensor_scalar(
+                out=mask_col[:], in0=v_col[:], scalar1=1.0, scalar2=0.0,
+                op0=ALU.add, op1=ALU.is_gt,
+            )
             nc.vector.tensor_scalar(
                 out=e_col[:], in0=e_col[:], scalar1=-0.5 * math.pi, scalar2=None, op0=ALU.add
             )
-            nc.vector.tensor_tensor(out=v_col[:], in0=r_col[:], in1=r_col[:], op=ALU.mult)
             nc.vector.tensor_scalar(
-                out=v_col[:], in0=v_col[:], scalar1=-1.0, scalar2=1.0,
-                op0=ALU.mult, op1=ALU.add,
-            )
-            nc.vector.tensor_scalar(
-                out=mask_col[:], in0=v_col[:], scalar1=0.0, scalar2=None, op0=ALU.is_gt
-            )
-            nc.vector.tensor_scalar(
-                out=v_col[:], in0=v_col[:], scalar1=1e-30, scalar2=None, op0=ALU.max
+                out=v_col[:], in0=v_col[:], scalar1=1.0, scalar2=1e-30, op0=ALU.add, op1=ALU.max
             )
 
         def params_tables():
@@ -352,9 +348,11 @@ def tile_linearrtus_kernel(
             for a in range(2):
                 cols = stage_cols(k, a)
                 nc.scalar.copy(out=st_c[:, :, cols], in_=ot_of[(k, a)][:])
-                if group_of[k][2] == "S":
+            if group_of[k][2] == "S":
+                for a in range(2):
+                    cols = stage_cols(k, a)
                     nc.scalar.activation(
-                        out=st_r[:, :, cols], in_=ot_of[(k, a)][:], func=ACT.Relu
+                        out=st_r[:, :, cols], in_=st_c[:, :, cols], func=ACT.Relu
                     )
 
         def vector_out(k):

import math
from contextlib import ExitStack

import concourse.mybir as mybir
from concourse.masks import make_identity

BF16 = mybir.dt.bfloat16
F32 = mybir.dt.float32
U32 = mybir.dt.uint32
U8 = mybir.dt.uint8
FP8X4 = mybir.dt.float8_e4m3fn_x4
ACT = mybir.ActivationFunctionType
ALU = mybir.AluOpType

FLOPS = 2 * 1024 * 1024 * 2048
P = 128
PI_SAFE = 3.1415925
CHUNKS = ((0, 0), (1, 0), (0, 1), (1, 1))
W_LATE_ENGINE = "g"
STORE_GROUPS = ((0, 2), (2, 2), (4, 2), (6, 2), (8, 2), (10, 2), (12, 2), (14, 2))
GROUP_RELU = "VSVSVSVS"
STAGE_BUFS = 4
CT_BUFS = 3


def tile_linearrtus_kernel(
    tc, h_c1, h_c2, x_t, r_param, theta_param, w1, w2, out_0, out_1, out_2
):
    nc = tc.nc
    with ExitStack() as ctx:
        const = ctx.enter_context(tc.tile_pool(name="const", bufs=1))
        grp_x = ctx.enter_context(tc.tile_pool(name="grp_x", bufs=2))
        grp_w = ctx.enter_context(tc.tile_pool(name="grp_w", bufs=4))
        work = ctx.enter_context(tc.tile_pool(name="work", bufs=CT_BUFS))
        stage = ctx.enter_context(tc.tile_pool(name="stage", bufs=STAGE_BUFS))
        psum = ctx.enter_context(tc.psum_pool(name="psum", bufs=1))
        ctx.enter_context(tc.manual_schedule())

        x_sb = [const.tile([P, 2048], BF16, name="x_sb%d" % ip) for ip in range(4)]
        h_first = [
            [const.tile([P, 4, 512], BF16, name="h%d_first%d" % (s, jc)) for jc in range(2)]
            for s in range(2)
        ]
        h_second = [const.tile([P, 4, 1024], BF16, name="h%d_second" % s) for s in range(2)]
        w_sb = [
            [const.tile([P, 8, 512], BF16, name="w%d_sb%d" % (m, jc)) for jc in range(2)]
            for m in range(2)
        ]
        x_codes = const.tile([P, 2, 1024], U32, name="x_codes", align_bytes=64)
        x_scales = const.tile([P, 2, 1024], U8, name="x_scales", align_bytes=64)
        w_codes = [
            const.tile([P, 2, 1024], U32, name="w1_codes", align_bytes=64),
            const.tile([P, 2, 1024], U32, name="w2_codes", align_bytes=64),
        ]
        w_scales = [
            const.tile([P, 2, 1024], U8, name="w1_scales", align_bytes=64),
            const.tile([P, 2, 1024], U8, name="w2_scales", align_bytes=64),
        ]
        ident_bf = const.tile([P, P], BF16, name="ident_bf")
        ident_f32 = const.tile([P, P], F32, name="ident_f32")
        par_rows = const.tile([P, P], BF16, name="par_rows")
        warm = const.tile([P, 8], F32, name="warm")
        r_col = const.tile([P, 8], F32, name="r_col")
        d_col = const.tile([P, 8], F32, name="d_col")
        e_col = const.tile([P, 8], F32, name="e_col")
        s1_col = const.tile([P, 8], F32, name="s1_col")
        s2_col = const.tile([P, 8], F32, name="s2_col")
        g_col = const.tile([P, 8], F32, name="g_col")
        phi_col = const.tile([P, 8], F32, name="phi_col")
        nphi_col = const.tile([P, 8], F32, name="nphi_col")
        v_col = const.tile([P, 8], F32, name="v_col")
        mask_col = const.tile([P, 8], F32, name="mask_col")
        sq_col = const.tile([P, 8], F32, name="sq_col")
        norm_col = const.tile([P, 8], F32, name="norm_col")

        nc.vector.memset(par_rows[:], 0.0)
        nc.vector.memset(warm[:], 0.0)
        nc.scalar.activation(out=warm[:], in_=warm[:], func=ACT.Sin)
        x_rows = x_t.rearrange("(p i) k -> p (i k)", i=8)
        h_rows = [
            h_c1.rearrange("(p i) c -> p i c", i=8),
            h_c2.rearrange("(p i) c -> p i c", i=8),
        ]
        w_in = [w1, w2]

        def load_x(ip):
            nc.sync.dma_start(out=x_sb[ip][:], in_=x_rows[:, 2048 * ip : 2048 * ip + 2048])

        def load_params():
            nc.sync.dma_start(
                out=par_rows[0:8, :], in_=r_param.rearrange("o (j p) -> (o j) p", p=P)
            )
            nc.sync.dma_start(
                out=par_rows[8:16, :], in_=theta_param.rearrange("o (j p) -> (o j) p", p=P)
            )

        def load_w(jc):
            cols = slice(512 * jc, 512 * jc + 512)
            for m in range(2):
                for g in range(2):
                    nc.sync.dma_start(
                        out=w_sb[m][jc][:, 4 * g : 4 * g + 4, :],
                        in_=w_in[m][512 * g : 512 * g + 512, cols].rearrange(
                            "(q e) c -> q e c", e=4
                        ),
                    )

        def load_h_first(jc):
            for s in range(2):
                nc.sync.dma_start(
                    out=h_first[s][jc][:], in_=h_rows[s][:, 0:4, 512 * jc : 512 * jc + 512]
                )

        def load_h_second():
            for s in range(2):
                nc.sync.dma_start(out=h_second[s][:], in_=h_rows[s][:, 4:8, :])

        load_x(0)
        load_params()
        load_x(1)
        load_w(0)
        load_x(2)
        load_x(3)
        load_h_first(0)
        load_w(1)
        load_h_second()
        load_h_first(1)

        make_identity(nc, ident_f32[:])
        make_identity(nc, ident_bf[:])

        def params_transpose():
            par_ps = psum.tile([P, P], BF16, name="par_ps", tag="o0")
            nc.tensor.transpose(par_ps[:], par_rows[:], ident_bf[:])
            return par_ps

        def params_angles(par_ps):
            nc.vector.tensor_copy(out=r_col[:], in_=par_ps[:, 0:8])
            nc.vector.tensor_scalar(
                out=d_col[:], in0=par_ps[:, 8:16], scalar1=-math.pi, scalar2=-PI_SAFE,
                op0=ALU.add, op1=ALU.max,
            )
            nc.vector.tensor_scalar(
                out=v_col[:], in0=r_col[:], scalar1=-1.0, scalar2=None, op0=ALU.mult
            )
            nc.vector.tensor_scalar(
                out=d_col[:], in0=d_col[:], scalar1=PI_SAFE, scalar2=None, op0=ALU.min
            )
            nc.vector.tensor_tensor(out=v_col[:], in0=v_col[:], in1=r_col[:], op=ALU.mult)
            nc.vector.scalar_tensor_tensor(
                out=e_col[:], in0=d_col[:], scalar=-1.0, in1=d_col[:], op0=ALU.mult, op1=ALU.max
            )
            nc.vector.tensor_scalar(
                out=mask_col[:], in0=v_col[:], scalar1=1.0, scalar2=0.0,
                op0=ALU.add, op1=ALU.is_gt,
            )
            nc.vector.tensor_scalar(
                out=e_col[:], in0=e_col[:], scalar1=-0.5 * math.pi, scalar2=None, op0=ALU.add
            )
            nc.vector.tensor_scalar(
                out=v_col[:], in0=v_col[:], scalar1=1.0, scalar2=1e-30, op0=ALU.add, op1=ALU.max
            )

        def params_tables():
            nc.scalar.activation(out=s1_col[:], in_=d_col[:], func=ACT.Sin)
            nc.scalar.activation(out=s2_col[:], in_=e_col[:], func=ACT.Sin)
            nc.scalar.activation(out=sq_col[:], in_=v_col[:], func=ACT.Sqrt)

        def params_finish():
            nc.vector.tensor_tensor(
                out=nphi_col[:], in0=r_col[:], in1=s1_col[:], op=ALU.mult
            )
            nc.vector.tensor_scalar(
                out=phi_col[:], in0=nphi_col[:], scalar1=-1.0, scalar2=None, op0=ALU.mult
            )
            nc.vector.tensor_tensor(out=g_col[:], in0=r_col[:], in1=s2_col[:], op=ALU.mult)
            nc.vector.tensor_tensor(
                out=norm_col[:], in0=sq_col[:], in1=mask_col[:], op=ALU.mult
            )

        x_words = [x_sb[ip][:].bitcast(F32) for ip in range(4)]

        def x_transposes(bh, g, half, bank):
            xt = psum.tile([P, 512], F32, name="xt", tag=bank)
            for i2 in range(2):
                for u in range(2):
                    c0 = 512 * i2 + 256 * g + u
                    nc.tensor.transpose(
                        xt[:, 128 * (2 * i2 + u) : 128 * (2 * i2 + u) + 128],
                        x_words[2 * bh + half][:, c0 : c0 + 255 : 2],
                        ident_f32[:],
                    )
            return xt

        def x_group_tile():
            xg = grp_x.tile([P, 2048], BF16, name="xg", tag="xg", align_bytes=64)
            return xg

        def x_copy(xg, half, xt):
            nc.scalar.copy(
                out=xg[:].bitcast(F32)[:, 512 * half : 512 * half + 512].rearrange(
                    "q (i p u) -> q i p u", i=2, p=P, u=2
                ),
                in_=xt[:].rearrange("q (i u p) -> q i p u", i=2, u=2, p=P),
            )

        def x_quant(bh, g, xg):
            cols = slice(512 * bh, 512 * bh + 512)
            nc.vector.quantize_mx(
                out=x_codes[:, g, cols].bitcast(FP8X4),
                scales=x_scales[:, g, cols],
                in_=xg[:],
            )

        def w_copy(m, g, jc, engine):
            wg = grp_w.tile([P, 512, 4], BF16, name="wg", tag="wg", align_bytes=64)
            dst = wg[:].rearrange("p (c i) t -> p c t i", i=4)
            src = w_sb[m][jc][:, 4 * g : 4 * g + 4, :].rearrange("p t (c i) -> p c t i", i=4)
            if engine == "v":
                nc.vector.tensor_copy(out=dst, in_=src)
            elif engine == "s":
                nc.scalar.copy(out=dst, in_=src)
            else:
                nc.gpsimd.tensor_scalar(
                    out=dst, in0=src, scalar1=1.0, scalar2=0.0, op0=ALU.mult, op1=ALU.add
                )
            return wg

        def w_quant(m, g, jc, wg):
            cols = slice(512 * jc, 512 * jc + 512)
            nc.vector.quantize_mx(
                out=w_codes[m][:, g, cols].bitcast(FP8X4),
                scales=w_scales[m][:, g, cols],
                in_=wg[:].rearrange("p c t -> p (c t)"),
            )

        units = [(c, m, jp) for c in range(4) for m in range(2) for jp in range(2)]
        n_units = len(units)
        ht_of = {}
        mm_of = {}
        ct_of = {}
        ot_of = {}
        st_of = {}

        def lane_block(k, a):
            c, m, jp = units[k]
            return 4 * CHUNKS[c][1] + 2 * jp + a

        def h_block(s, bh, il, j):
            if bh == 0:
                return h_first[s][j // 4][:, il, 128 * (j % 4) : 128 * (j % 4) + 128]
            return h_second[s][:, il, 128 * j : 128 * j + 128]

        def h_transposes(c, jl):
            bh, jc = CHUNKS[c]
            ht = psum.tile([P, 2, 512], BF16, name="ht", tag="h%d" % jl)
            for s in range(2):
                for il in range(4):
                    if c < 3:
                        nc.tensor.matmul(
                            ht[:, s, 128 * il : 128 * il + 128],
                            lhsT=h_block(s, bh, il, 4 * jc + jl),
                            rhs=ident_bf[:],
                            start=True,
                            stop=True,
                        )
                    else:
                        nc.tensor.transpose(
                            ht[:, s, 128 * il : 128 * il + 128],
                            h_block(s, bh, il, 4 * jc + jl),
                            ident_bf[:],
                        )
            ht_of[(c, jl)] = ht

        def mx_passes(k, a):
            c, m, jp = units[k]
            bh = CHUNKS[c][0]
            j = lane_block(k, a)
            h_cols = slice(128 * j, 128 * j + 128)
            b_cols = slice(512 * bh, 512 * bh + 512)
            mm = psum.tile([P, 512], F32, name="mm", tag="m%d" % a)
            for g in range(2):
                nc.tensor.matmul_mx(
                    out=mm[:],
                    lhsT=w_codes[m][:, g, h_cols].bitcast(FP8X4),
                    lhsT_scale=w_scales[m][:, g, h_cols],
                    rhs=x_codes[:, g, b_cols].bitcast(FP8X4),
                    rhs_scale=x_scales[:, g, b_cols],
                    start=(g == 0),
                    stop=(g == 1),
                )
            mm_of[(k, a)] = mm

        def scale_out(k, a):
            j = lane_block(k, a)
            ct = work.tile([P, 512], F32, name="ct%d" % a, tag="ct%d" % a)
            nc.scalar.activation(
                out=ct[:], in_=mm_of[(k, a)][:], func=ACT.Copy, scale=norm_col[:, j : j + 1]
            )
            ct_of[(k, a)] = ct

        plan = (((0, g_col), (1, nphi_col)), ((1, g_col), (0, phi_col)))

        def rotate_add(k):
            c, m, jp = units[k]
            for s, coef in plan[m]:
                for a in range(2):
                    j = lane_block(k, a)
                    ct = ct_of[(k, a)]
                    nc.vector.scalar_tensor_tensor(
                        out=ct[:], in0=ht_of[(c, 2 * jp + a)][:, s, :],
                        scalar=coef[:, j : j + 1], in1=ct[:], op0=ALU.mult, op1=ALU.add,
                    )

        def back_transposes(k, a):
            ot = psum.tile([P, 4, P], F32, name="ot", tag="o%d" % a)
            for il in range(4):
                nc.tensor.transpose(
                    ot[:, il, :], ct_of[(k, a)][:, 128 * il : 128 * il + 128], ident_f32[:]
                )
            ot_of[(k, a)] = ot

        group_of = {}
        for index, (first, count) in enumerate(STORE_GROUPS):
            for k in range(first, first + count):
                group_of[k] = (first, count, GROUP_RELU[index])

        def stage_tiles(k):
            first, count, who = group_of[k]
            if first not in st_of:
                st_of[first] = [
                    stage.tile([P, 4, 256 * count], F32, name="st_c", tag="c"),
                    stage.tile([P, 4, 256 * count], F32, name="st_r", tag="r"),
                ]
            return st_of[first]

        def stage_cols(k, a):
            lo = 128 * (2 * (k - group_of[k][0]) + a)
            return slice(lo, lo + 128)

        def scalar_out(k):
            st_c, st_r = stage_tiles(k)
            if k == n_units - 1:
                cols = stage_cols(k, 0)
                nc.scalar.copy(out=st_c[:, :, cols], in_=ot_of[(k, 0)][:])
                nc.scalar.activation(out=st_r[:, :, cols], in_=ot_of[(k, 0)][:], func=ACT.Relu)
                return
            for a in range(2):
                cols = stage_cols(k, a)
                nc.scalar.copy(out=st_c[:, :, cols], in_=ot_of[(k, a)][:])
            if group_of[k][2] == "S":
                for a in range(2):
                    cols = stage_cols(k, a)
                    nc.scalar.activation(
                        out=st_r[:, :, cols], in_=st_c[:, :, cols], func=ACT.Relu
                    )

        def vector_out(k):
            first, count, who = group_of[k]
            st_c, st_r = stage_tiles(k)
            if k == n_units - 1:
                cols = stage_cols(k, 1)
                nc.vector.tensor_copy(out=st_c[:, :, cols], in_=ot_of[(k, 1)][:])
                nc.vector.tensor_scalar(
                    out=st_r[:, :, cols], in0=ot_of[(k, 1)][:],
                    scalar1=0.0, scalar2=None, op0=ALU.max,
                )
            elif who == "V" and k == first + count - 1:
                nc.vector.tensor_scalar(
                    out=st_r[:], in0=st_c[:], scalar1=0.0, scalar2=None, op0=ALU.max
                )

        c_rows = [
            out_0.rearrange("(p i) c -> p i c", i=8),
            out_1.rearrange("(p i) c -> p i c", i=8),
        ]
        r_rows = out_2.rearrange("(p i) c -> p i c", i=8)

        def stores(k):
            first, count, who = group_of[k]
            if k != first + count - 1:
                return
            c, m, jp = units[first]
            bh = CHUNKS[c][0]
            base = 128 * lane_block(first, 0)
            st_c, st_r = stage_tiles(k)
            rows = slice(4 * bh, 4 * bh + 4)
            nc.sync.dma_start(out=c_rows[m][:, rows, base : base + 256 * count], in_=st_c[:])
            nc.sync.dma_start(
                out=r_rows[:, rows, 1024 * m + base : 1024 * m + base + 256 * count], in_=st_r[:]
            )

        xt_a = x_transposes(0, 0, 0, "m0")
        xt_c = x_transposes(0, 1, 0, "h0")
        par_ps = params_transpose()
        xt_b = x_transposes(0, 0, 1, "m1")
        xt_d = x_transposes(0, 1, 1, "h1")
        params_angles(par_ps)
        xg00 = x_group_tile()
        xg01 = x_group_tile()
        x_copy(xg00, 0, xt_a)
        x_copy(xg01, 0, xt_c)
        x_copy(xg00, 1, xt_b)
        x_copy(xg01, 1, xt_d)
        wg_a = w_copy(0, 0, 0, "v")
        wg_b = w_copy(0, 1, 0, "s")
        params_tables()
        x_quant(0, 0, xg00)
        w_quant(0, 0, 0, wg_a)
        wg_c = w_copy(1, 0, 0, "v")
        x_quant(0, 1, xg01)
        w_quant(0, 1, 0, wg_b)
        params_finish()
        wg_d = w_copy(1, 1, 0, "v")
        w_quant(1, 0, 0, wg_c)
        w_quant(1, 1, 0, wg_d)

        xt_a = x_transposes(1, 0, 0, "o0")
        xt_b = x_transposes(1, 0, 1, "o1")
        mx_passes(0, 0)
        mx_passes(0, 1)
        h_transposes(0, 0)
        h_transposes(0, 1)
        xg10 = x_group_tile()
        x_copy(xg10, 0, xt_a)
        x_copy(xg10, 1, xt_b)
        scale_out(0, 0)
        scale_out(0, 1)
        mx_passes(1, 0)
        mx_passes(1, 1)
        h_transposes(0, 2)
        h_transposes(0, 3)
        xt_c = x_transposes(1, 1, 0, "o0")
        xt_d = x_transposes(1, 1, 1, "o1")
        scale_out(1, 0)
        scale_out(1, 1)
        xg11 = x_group_tile()
        x_copy(xg11, 0, xt_c)
        x_copy(xg11, 1, xt_d)
        x_quant(1, 0, xg10)

        late = ((0, 0), (0, 1), (1, 0), (1, 1))
        late_wg = {}
        for t in range(n_units + 1):
            if t >= 1:
                if t + 1 < n_units:
                    mx_passes(t + 1, 0)
                    mx_passes(t + 1, 1)
                back_transposes(t - 1, 0)
                back_transposes(t - 1, 1)
                c, m, jp = units[t - 1]
                if m == 1 and c + 1 < 4:
                    h_transposes(c + 1, 2 * jp)
                    h_transposes(c + 1, 2 * jp + 1)
                if t + 1 < n_units:
                    scale_out(t + 1, 0)
                    scale_out(t + 1, 1)
                scalar_out(t - 1)
            if 2 <= t <= 5:
                late_wg[t - 2] = w_copy(late[t - 2][0], late[t - 2][1], 1, W_LATE_ENGINE)
            if t < n_units:
                rotate_add(t)
            if t == 1:
                x_quant(1, 1, xg11)
            if 3 <= t <= 5:
                w_quant(late[t - 3][0], late[t - 3][1], 1, late_wg[t - 3])
            if t == 5:
                w_quant(late[3][0], late[3][1], 1, late_wg[3])
            done = [t - 2] if t < n_units else [t - 2, t - 1]
            for k in done:
                if k >= 0:
                    vector_out(k)
                    stores(k)
